import numpy as np
import ml_dtypes


def mxq(x, axis, fmt="e4m3"):
    dtype, down = {"e4m3": (ml_dtypes.float8_e4m3fn, 7), "e5m2": (ml_dtypes.float8_e5m2, 14)}[fmt]
    v = np.moveaxis(np.asarray(x, np.float32).astype(ml_dtypes.bfloat16).astype(np.float64), axis, -1)
    blocks = v.reshape(v.shape[:-1] + (-1, 32))
    amax = np.abs(blocks).max(-1, keepdims=True)
    byte = np.maximum(np.where(amax > 0, np.frexp(amax)[1] - 1 + 127, 0) - down, 1)
    scale = np.exp2(byte - 127.0)
    codes = (blocks / scale).astype(np.float32).astype(dtype).astype(np.float64)
    return np.moveaxis((codes * scale).reshape(v.shape), -1, axis)


WIDE = False


def mx_kscale(k):
    if not WIDE:
        return np.ones(k)
    levels = np.array([10, -10, 5, -5, 0])
    a = np.random.permutation(np.resize(levels, k // 512 * 4)).reshape(k // 512, 4)
    idx = np.arange(k)
    return np.exp2(a[idx // 512, idx % 128 // 32])


BF16 = ml_dtypes.bfloat16


def bf(x):
    return np.asarray(x, np.float32).astype(BF16)


def f64(x):
    return np.asarray(x).astype(np.float64)


E2M1 = np.array([0.0, 0.5, 1.0, 1.5, 2.0, 3.0, 4.0, 6.0, -0.0, -0.5, -1.0, -1.5, -2.0, -3.0, -4.0, -6.0])


def pack_weight(w, fmt):
    k, n = w.shape
    w = f64(bf(w)).reshape(k // 32, 32, n)
    amax = np.abs(w).max(1)
    if fmt == "e4m3":
        byte = np.frexp(amax)[1] - 1 + 127 - 7
    else:
        mant, ex = np.frexp(amax / 6.0)
        byte = np.where(mant > 0.5, ex, ex - 1) + 127
    byte = np.clip(np.where(amax > 0, byte, 1), 1, 254)
    scaled = (w * np.exp2(127.0 - byte)[:, None, :]).reshape(k, n).astype(np.float32)
    by_word = np.ascontiguousarray(scaled.reshape(k // 512, 128, 4, n).transpose(0, 1, 3, 2))
    if fmt == "e4m3":
        words = by_word.astype(ml_dtypes.float8_e4m3fn).view(np.uint8)
    else:
        c = by_word.astype(ml_dtypes.float4_e2m1fn).view(np.uint8) & 0xF
        words = c[..., 0::2] | (c[..., 1::2] << 4)
    return np.ascontiguousarray(words), np.ascontiguousarray(byte.astype(np.uint8).reshape(k // 512, 16, n))


def unpack_weight(words, scales, fmt):
    g, p, n, _ = words.shape
    if fmt == "e4m3":
        vals = np.ascontiguousarray(words).view(ml_dtypes.float8_e4m3fn).astype(np.float64)
    else:
        nib = np.empty((g, p, n, 4), np.uint8)
        nib[..., 0::2] = words & 0xF
        nib[..., 1::2] = words >> 4
        vals = E2M1[nib]
    vals = vals * np.repeat(np.exp2(scales.astype(np.float64) - 127.0), 8, axis=1)[..., None]
    return vals.transpose(0, 1, 3, 2).reshape(g * 512, n)


B, TW, C, MS, RED = 2, 64, 256, 4, 16
T = TW * MS
D = C * MS
F = D * RED


def sigmoid(v):
    return 1.0 / (1.0 + np.exp(-v))


def setup_inputs():
    t = mx_kscale(F)
    x = bf(np.random.standard_normal((B, T, C)))
    w1_words, w1_scales = pack_weight(np.random.standard_normal((D, F)) / np.sqrt(D) * t, "e4m3")
    w2_words, w2_scales = pack_weight(np.random.standard_normal((F, D)) * 3.0 / np.sqrt(F) / t[:, None], "e4m3")
    return {"x": x,
            "w1_words": w1_words, "w1_scales": w1_scales,
            "w2_words": w2_words, "w2_scales": w2_scales}


def reference(x, w1_words, w1_scales, w2_words, w2_scales):
    xt = f64(x).reshape(B, TW, MS, C).swapaxes(-1, -2)
    flat = xt.reshape(B, TW, D)
    h = np.maximum(mxq(flat, 2, "e4m3") @ unpack_weight(w1_words, w1_scales, "e4m3"), 0.0)
    a = mxq(h, 2, "e4m3") @ unpack_weight(w2_words, w2_scales, "e4m3")
    g = sigmoid(a).reshape(B, TW, C, MS)
    e = np.exp(g - g.max(-1, keepdims=True))
    y = e / e.sum(-1, keepdims=True)
    return (xt * y).sum(-1)

@@ -1,0 +1,221 @@
+from contextlib import ExitStack
+
+import concourse.mybir as mybir
+from concourse.masks import make_identity
+
+F32 = mybir.dt.float32
+BF16 = mybir.dt.bfloat16
+I32 = mybir.dt.int32
+U32 = mybir.dt.uint32
+U8 = mybir.dt.uint8
+FP8X4 = mybir.dt.float8_e4m3fn_x4
+ACT = mybir.ActivationFunctionType
+ALU = mybir.AluOpType
+
+P = 128
+PACK = 4
+K_PASS = P * PACK
+N_TILE = 512
+
+TOKENS = 128
+MS = 4
+C = 256
+D = C * MS
+F = D * 16
+D_PASSES = D // K_PASS
+F_GROUPS = F // K_PASS
+
+QUADS = 4
+PLANES = 4
+ROWS = 4
+
+UNIT = 2
+UNITS = F_GROUPS // UNIT
+CHUNK = 4
+CHUNKS = F_GROUPS // CHUNK
+W1_BUFS = 6
+W2_BUFS = 16
+HALVES = D // N_TILE
+C_HALF = C // HALVES
+
+FLOPS = 2 * TOKENS * D * F * 2
+
+
+def tile_dwamformer_pa_k_kernel(tc, x, w1_words, w1_scales, w2_words, w2_scales, out):
+    nc = tc.nc
+    with ExitStack() as ctx:
+        ctx.enter_context(tc.manual_schedule())
+        keep = ctx.enter_context(tc.tile_pool(name="keep", bufs=1))
+        w1_pool = ctx.enter_context(tc.tile_pool(name="w1_pool", bufs=W1_BUFS))
+        w2_pool = ctx.enter_context(tc.tile_pool(name="w2_pool", bufs=W2_BUFS))
+        stage = ctx.enter_context(tc.tile_pool(name="stage", bufs=2))
+        psum_h = ctx.enter_context(tc.psum_pool(name="psum_h", bufs=2 * UNIT))
+        psum_t = ctx.enter_context(tc.psum_pool(name="psum_t", bufs=2))
+        psum_a = ctx.enter_context(tc.psum_pool(name="psum_a", bufs=1))
+
+        x_rows = x.rearrange("b (w m) c -> (b w) m c", m=MS)
+        w1_rows = w1_words.rearrange("g p n t -> p g (n t)")
+        w2_rows = w2_words.rearrange("g p n t -> p g (n t)")
+        out_rows = out.rearrange("b w c -> (b w) c")
+
+        ident = keep.tile([P, P], BF16)
+        x_tok = keep.tile([P, MS, C], BF16)
+        flat_grouped = keep.tile([P, D_PASSES, TOKENS, PACK], BF16, align_bytes=64)
+        flat_codes = keep.tile([P, D_PASSES, TOKENS], U32, align_bytes=64)
+        flat_scales = keep.tile([P, D_PASSES, TOKENS], U8, align_bytes=64)
+        h_codes = keep.tile([P, F_GROUPS, TOKENS], U32, align_bytes=64)
+        h_scales = keep.tile([P, F_GROUPS, TOKENS], U8, align_bytes=64)
+        w1_planes = keep.tile([P, D_PASSES, F // PLANES], U8, align_bytes=64)
+        w2_planes = keep.tile([P, F_GROUPS // PLANES, D], U8, align_bytes=64)
+        warm = keep.tile([P, 1], F32)
+        result = keep.tile([P, C], F32)
+
+        nc.vector.memset(warm[:], 0.0)
+        nc.vector.memset(w1_planes[:].bitcast(I32), 0)
+        nc.vector.memset(w2_planes[:].bitcast(I32), 0)
+        nc.scalar.activation(out=warm[:], in_=warm[:], func=ACT.Tanh)
+        make_identity(nc, ident[:])
+
+        def load_w1(chunk):
+            words = w1_pool.tile([P, D_PASSES, CHUNK * N_TILE], U32, name="w1_chunk", align_bytes=64)
+            first = chunk * CHUNK * N_TILE * PACK
+            nc.sync.dma_start(
+                out=words[:].bitcast(I32),
+                in_=w1_rows[:, :, first : first + CHUNK * N_TILE * PACK].bitcast(I32),
+            )
+            return words
+
+        def load_w2(group):
+            words = w2_pool.tile([P, D], U32, name="w2_group", align_bytes=64)
+            nc.sync.dma_start(out=words[:].bitcast(I32), in_=w2_rows[:, group, :].bitcast(I32))
+            return words
+
+        def load_planes(planes, rows_of):
+            for quad in range(QUADS):
+                for r in range(ROWS):
+                    first = 32 * quad + r
+                    nc.sync.dma_start(
+                        out=planes[first : first + PLANES * ROWS : ROWS, :, :].bitcast(I32),
+                        in_=rows_of(ROWS * quad + r).bitcast(I32),
+                    )
+
+        nc.sync.dma_start(out=x_tok[:], in_=x_rows)
+        w1_chunks = {}
+        w1_chunks[0] = load_w1(0)
+        load_planes(w1_planes, lambda q: w1_scales[:, q, :].rearrange("g (k n) -> k g n", k=PLANES))
+        for chunk in range(1, W1_BUFS):
+            w1_chunks[chunk] = load_w1(chunk)
+
+        xt_bank = psum_t.tile([P, D_PASSES, MS, TOKENS], BF16, name="t_bank")
+        for g in range(D_PASSES):
+            for m in range(MS):
+                nc.tensor.transpose(xt_bank[:, g, m, :], x_tok[:, m, g * P : (g + 1) * P], ident[:])
+        nc.vector.tensor_copy(out=flat_grouped[:], in_=xt_bank[:].rearrange("p g m w -> p g w m"))
+        nc.vector.quantize_mx(
+            out=flat_codes[:].rearrange("p g w -> p (g w)").bitcast(FP8X4),
+            scales=flat_scales[:].rearrange("p g w -> p (g w)"),
+            in_=flat_grouped[:].rearrange("p g w m -> p (g w m)"),
+        )
+
+        def hidden(unit):
+            h_sorted = stage.tile([P, UNIT, PACK, P], BF16, name="h_sorted")
+            for i in range(UNIT):
+                group = unit * UNIT + i
+                words = w1_chunks[group // CHUNK]
+                cols = slice((group % CHUNK) * N_TILE, (group % CHUNK + 1) * N_TILE)
+                per_plane = F_GROUPS // PLANES
+                plane = ROWS * (group // per_plane)
+                plane_cols = slice((group % per_plane) * N_TILE, (group % per_plane + 1) * N_TILE)
+                h_bank = psum_h.tile([P, N_TILE], F32, name="h_bank")
+                for g in range(D_PASSES):
+                    nc.tensor.matmul_mx(
+                        out=h_bank[:],
+                        lhsT=flat_codes[:, g, :].bitcast(FP8X4),
+                        lhsT_scale=flat_scales[:, g, :],
+                        rhs=words[:, g, cols].bitcast(FP8X4),
+                        rhs_scale=w1_planes[plane:P, g, plane_cols],
+                        start=(g == 0),
+                        stop=(g == D_PASSES - 1),
+                    )
+                nc.scalar.activation(
+                    out=h_sorted[:, i, :, :],
+                    in_=h_bank[:].rearrange("p (q t) -> p t q", t=PACK),
+                    func=ACT.Relu,
+                )
+            return h_sorted
+
+        def transpose_and_quantise(unit, h_sorted):
+            t_bank = psum_t.tile([P, UNIT, PACK, TOKENS], BF16, name="t_bank")
+            for i in range(UNIT):
+                for t in range(PACK):
+                    nc.tensor.transpose(t_bank[:, i, t, :], h_sorted[:, i, t, :], ident[:])
+            h_grouped = stage.tile([P, UNIT, TOKENS, PACK], BF16, name="h_grouped", align_bytes=64)
+            nc.vector.tensor_copy(out=h_grouped[:], in_=t_bank[:].rearrange("p i t w -> p i w t"))
+            groups = slice(unit * UNIT, (unit + 1) * UNIT)
+            nc.vector.quantize_mx(
+                out=h_codes[:, groups, :].rearrange("p i w -> p (i w)").bitcast(FP8X4),
+                scales=h_scales[:, groups, :].rearrange("p i w -> p (i w)"),
+                in_=h_grouped[:].rearrange("p i w t -> p (i w t)"),
+            )
+
+        w2_groups = {}
+        units_per_chunk = CHUNK // UNIT
+        previous = None
+        for unit in range(UNITS):
+            h_sorted = hidden(unit)
+            if previous is not None:
+                transpose_and_quantise(unit - 1, previous)
+            previous = h_sorted
+            if unit % units_per_chunk == units_per_chunk - 1:
+                chunk = unit // units_per_chunk + W1_BUFS
+                if chunk < CHUNKS:
+                    w1_chunks[chunk] = load_w1(chunk)
+                if chunk == CHUNKS - 1:
+                    load_planes(
+                        w2_planes, lambda q: w2_scales[:, q, :].rearrange("(a k) n -> k a n", k=PLANES)
+                    )
+                    for group in range(W2_BUFS):
+                        w2_groups[group] = load_w2(group)
+        transpose_and_quantise(UNITS - 1, previous)
+
+        a_banks = [psum_a.tile([P, N_TILE], F32, name="a_bank%d" % half) for half in range(HALVES)]
+        for group in range(F_GROUPS):
+            words = w2_groups[group]
+            for half in range(HALVES):
+                cols = slice(half * N_TILE, (half + 1) * N_TILE)
+                nc.tensor.matmul_mx(
+                    out=a_banks[half][:],
+                    lhsT=h_codes[:, group, :].bitcast(FP8X4),
+                    lhsT_scale=h_scales[:, group, :],
+                    rhs=words[:, cols].bitcast(FP8X4),
+                    rhs_scale=w2_planes[ROWS * (group % PLANES) : P, group // PLANES, cols],
+                    start=(group == 0),
+                    stop=(group == F_GROUPS - 1),
+                )
+            if group + W2_BUFS < F_GROUPS:
+                w2_groups[group + W2_BUFS] = load_w2(group + W2_BUFS)
+
+        for half in range(HALVES):
+            chans = slice(half * C_HALF, (half + 1) * C_HALF)
+            gate = stage.tile([P, MS, C_HALF], F32, name="gate")
+            nc.scalar.activation(
+                out=gate[:],
+                in_=a_banks[half][:].rearrange("p (c m) -> p m c", m=MS),
+                func=ACT.Tanh,
+                scale=0.5,
+            )
+            expo = stage.tile([P, MS, C_HALF], F32, name="expo")
+            nc.scalar.activation(out=expo[:], in_=gate[:], func=ACT.Exp, scale=0.5)
+            weighted = stage.tile([P, MS, C_HALF], F32, name="weighted")
+            nc.vector.tensor_tensor(out=weighted[:], in0=expo[:], in1=x_tok[:, :, chans], op=ALU.mult)
+            top = stage.tile([P, C_HALF], F32, name="top")
+            nc.vector.tensor_reduce(
+                out=top[:], in_=weighted[:].rearrange("p m c -> p c m"), axis=mybir.AxisListType.X, op=ALU.add
+            )
+            bottom = stage.tile([P, C_HALF], F32, name="bottom")
+            nc.vector.tensor_reduce(
+                out=bottom[:], in_=expo[:].rearrange("p m c -> p c m"), axis=mybir.AxisListType.X, op=ALU.add
+            )
+            nc.vector.reciprocal(out=bottom[:], in_=bottom[:])
+            nc.vector.tensor_tensor(out=result[:, chans], in0=top[:], in1=bottom[:], op=ALU.mult)
+        nc.sync.dma_start(out=out_rows, in_=result[:])

@@ -35,6 +35,7 @@ CHUNK = 4
 CHUNKS = F_GROUPS // CHUNK
 W1_BUFS = 6
 W2_BUFS = 16
+TAIL = 8
 HALVES = D // N_TILE
 C_HALF = C // HALVES
 
@@ -68,7 +69,6 @@ def tile_dwamformer_pa_k_kernel(tc, x, w1_words, w1_scales, w2_words, w2_scales,
         w1_planes = keep.tile([P, D_PASSES, F // PLANES], U8, align_bytes=64)
         w2_planes = keep.tile([P, F_GROUPS // PLANES, D], U8, align_bytes=64)
         warm = keep.tile([P, 1], F32)
-        result = keep.tile([P, C], F32)
 
         nc.vector.memset(warm[:], 0.0)
         nc.vector.memset(w1_planes[:].bitcast(I32), 0)
@@ -85,9 +85,13 @@ def tile_dwamformer_pa_k_kernel(tc, x, w1_words, w1_scales, w2_words, w2_scales,
             )
             return words
 
-        def load_w2(group):
-            words = w2_pool.tile([P, D], U32, name="w2_group", align_bytes=64)
-            nc.sync.dma_start(out=words[:].bitcast(I32), in_=w2_rows[:, group, :].bitcast(I32))
+        def load_w2(piece):
+            group, first_half, end_half = piece
+            words = w2_pool.tile([P, (end_half - first_half) * N_TILE], U32, name="w2_piece", align_bytes=64)
+            nc.sync.dma_start(
+                out=words[:].bitcast(I32),
+                in_=w2_rows[:, group, first_half * N_TILE * PACK : end_half * N_TILE * PACK].bitcast(I32),
+            )
             return words
 
         def load_planes(planes, rows_of):
@@ -158,7 +162,10 @@ def tile_dwamformer_pa_k_kernel(tc, x, w1_words, w1_scales, w2_words, w2_scales,
                 in_=h_grouped[:].rearrange("p i w t -> p (i w t)"),
             )
 
-        w2_groups = {}
+        pieces = [(group, 0, HALVES) for group in range(F_GROUPS - TAIL)]
+        for half in range(HALVES):
+            pieces.extend([(group, half, half + 1) for group in range(F_GROUPS - TAIL, F_GROUPS)])
+        w2_loaded = {}
         units_per_chunk = CHUNK // UNIT
         previous = None
         for unit in range(UNITS):
@@ -174,35 +181,15 @@ def tile_dwamformer_pa_k_kernel(tc, x, w1_words, w1_scales, w2_words, w2_scales,
                     load_planes(
                         w2_planes, lambda q: w2_scales[:, q, :].rearrange("(a k) n -> k a n", k=PLANES)
                     )
-                    for group in range(W2_BUFS):
-                        w2_groups[group] = load_w2(group)
+                    for index in range(W2_BUFS):
+                        w2_loaded[index] = load_w2(pieces[index])
         transpose_and_quantise(UNITS - 1, previous)
 
-        a_banks = [psum_a.tile([P, N_TILE], F32, name="a_bank%d" % half) for half in range(HALVES)]
-        for group in range(F_GROUPS):
-            words = w2_groups[group]
-            for half in range(HALVES):
-                cols = slice(half * N_TILE, (half + 1) * N_TILE)
-                nc.tensor.matmul_mx(
-                    out=a_banks[half][:],
-                    lhsT=h_codes[:, group, :].bitcast(FP8X4),
-                    lhsT_scale=h_scales[:, group, :],
-                    rhs=words[:, cols].bitcast(FP8X4),
-                    rhs_scale=w2_planes[ROWS * (group % PLANES) : P, group // PLANES, cols],
-                    start=(group == 0),
-                    stop=(group == F_GROUPS - 1),
-                )
-            if group + W2_BUFS < F_GROUPS:
-                w2_groups[group + W2_BUFS] = load_w2(group + W2_BUFS)
-
-        for half in range(HALVES):
+        def pool_windows(half, a_bank):
             chans = slice(half * C_HALF, (half + 1) * C_HALF)
             gate = stage.tile([P, MS, C_HALF], F32, name="gate")
             nc.scalar.activation(
-                out=gate[:],
-                in_=a_banks[half][:].rearrange("p (c m) -> p m c", m=MS),
-                func=ACT.Tanh,
-                scale=0.5,
+                out=gate[:], in_=a_bank[:].rearrange("p (c m) -> p m c", m=MS), func=ACT.Tanh, scale=0.5
             )
             expo = stage.tile([P, MS, C_HALF], F32, name="expo")
             nc.scalar.activation(out=expo[:], in_=gate[:], func=ACT.Exp, scale=0.5)
@@ -217,5 +204,27 @@ def tile_dwamformer_pa_k_kernel(tc, x, w1_words, w1_scales, w2_words, w2_scales,
                 out=bottom[:], in_=expo[:].rearrange("p m c -> p c m"), axis=mybir.AxisListType.X, op=ALU.add
             )
             nc.vector.reciprocal(out=bottom[:], in_=bottom[:])
-            nc.vector.tensor_tensor(out=result[:, chans], in0=top[:], in1=bottom[:], op=ALU.mult)
-        nc.sync.dma_start(out=out_rows, in_=result[:])
+            result = stage.tile([P, C_HALF], F32, name="result")
+            nc.vector.tensor_tensor(out=result[:], in0=top[:], in1=bottom[:], op=ALU.mult)
+            nc.sync.dma_start(out=out_rows[:, chans], in_=result[:])
+
+        a_banks = [psum_a.tile([P, N_TILE], F32, name="a_bank%d" % half) for half in range(HALVES)]
+        for index, (group, first_half, end_half) in enumerate(pieces):
+            words = w2_loaded[index]
+            for half in range(first_half, end_half):
+                nc.tensor.matmul_mx(
+                    out=a_banks[half][:],
+                    lhsT=h_codes[:, group, :].bitcast(FP8X4),
+                    lhsT_scale=h_scales[:, group, :],
+                    rhs=words[:, (half - first_half) * N_TILE : (half - first_half + 1) * N_TILE].bitcast(FP8X4),
+                    rhs_scale=w2_planes[
+                        ROWS * (group % PLANES) : P, group // PLANES, half * N_TILE : (half + 1) * N_TILE
+                    ],
+                    start=(group == 0),
+                    stop=(group == F_GROUPS - 1),
+                )
+            if index + W2_BUFS < len(pieces):
+                w2_loaded[index + W2_BUFS] = load_w2(pieces[index + W2_BUFS])
+            if group == F_GROUPS - 1:
+                for half in range(first_half, end_half):
+                    pool_windows(half, a_banks[half])

@@ -34,7 +34,8 @@ UNITS = F_GROUPS // UNIT
 CHUNK = 4
 CHUNKS = F_GROUPS // CHUNK
 W1_BUFS = 6
-W2_BUFS = 16
+W2_GROUPS = 2
+W2_BUFS = 8
 TAIL = 8
 HALVES = D // N_TILE
 C_HALF = C // HALVES
@@ -86,11 +87,15 @@ def tile_dwamformer_pa_k_kernel(tc, x, w1_words, w1_scales, w2_words, w2_scales,
             return words
 
         def load_w2(piece):
-            group, first_half, end_half = piece
-            words = w2_pool.tile([P, (end_half - first_half) * N_TILE], U32, name="w2_piece", align_bytes=64)
+            first, first_half, end_half = piece
+            words = w2_pool.tile(
+                [P, W2_GROUPS, (end_half - first_half) * N_TILE], U32, name="w2_piece", align_bytes=64
+            )
             nc.sync.dma_start(
                 out=words[:].bitcast(I32),
-                in_=w2_rows[:, group, first_half * N_TILE * PACK : end_half * N_TILE * PACK].bitcast(I32),
+                in_=w2_rows[
+                    :, first : first + W2_GROUPS, first_half * N_TILE * PACK : end_half * N_TILE * PACK
+                ].bitcast(I32),
             )
             return words
 
@@ -162,9 +167,9 @@ def tile_dwamformer_pa_k_kernel(tc, x, w1_words, w1_scales, w2_words, w2_scales,
                 in_=h_grouped[:].rearrange("p i w t -> p (i w t)"),
             )
 
-        pieces = [(group, 0, HALVES) for group in range(F_GROUPS - TAIL)]
+        pieces = [(first, 0, HALVES) for first in range(0, F_GROUPS - TAIL, W2_GROUPS)]
         for half in range(HALVES):
-            pieces.extend([(group, half, half + 1) for group in range(F_GROUPS - TAIL, F_GROUPS)])
+            pieces.extend([(first, half, half + 1) for first in range(F_GROUPS - TAIL, F_GROUPS, W2_GROUPS)])
         w2_loaded = {}
         units_per_chunk = CHUNK // UNIT
         previous = None
@@ -209,22 +214,25 @@ def tile_dwamformer_pa_k_kernel(tc, x, w1_words, w1_scales, w2_words, w2_scales,
             nc.sync.dma_start(out=out_rows[:, chans], in_=result[:])
 
         a_banks = [psum_a.tile([P, N_TILE], F32, name="a_bank%d" % half) for half in range(HALVES)]
-        for index, (group, first_half, end_half) in enumerate(pieces):
+        for index, (first, first_half, end_half) in enumerate(pieces):
             words = w2_loaded[index]
-            for half in range(first_half, end_half):
-                nc.tensor.matmul_mx(
-                    out=a_banks[half][:],
-                    lhsT=h_codes[:, group, :].bitcast(FP8X4),
-                    lhsT_scale=h_scales[:, group, :],
-                    rhs=words[:, (half - first_half) * N_TILE : (half - first_half + 1) * N_TILE].bitcast(FP8X4),
-                    rhs_scale=w2_planes[
-                        ROWS * (group % PLANES) : P, group // PLANES, half * N_TILE : (half + 1) * N_TILE
-                    ],
-                    start=(group == 0),
-                    stop=(group == F_GROUPS - 1),
-                )
+            for i in range(W2_GROUPS):
+                group = first + i
+                for half in range(first_half, end_half):
+                    cols = slice((half - first_half) * N_TILE, (half - first_half + 1) * N_TILE)
+                    nc.tensor.matmul_mx(
+                        out=a_banks[half][:],
+                        lhsT=h_codes[:, group, :].bitcast(FP8X4),
+                        lhsT_scale=h_scales[:, group, :],
+                        rhs=words[:, i, cols].bitcast(FP8X4),
+                        rhs_scale=w2_planes[
+                            ROWS * (group % PLANES) : P, group // PLANES, half * N_TILE : (half + 1) * N_TILE
+                        ],
+                        start=(group == 0),
+                        stop=(group == F_GROUPS - 1),
+                    )
             if index + W2_BUFS < len(pieces):
                 w2_loaded[index + W2_BUFS] = load_w2(pieces[index + W2_BUFS])
-            if group == F_GROUPS - 1:
+            if first + W2_GROUPS == F_GROUPS:
                 for half in range(first_half, end_half):
                     pool_windows(half, a_banks[half])

@@ -39,6 +39,8 @@ W2_BUFS = 8
 TAIL = 8
 HALVES = D // N_TILE
 C_HALF = C // HALVES
+PARTS = 2
+C_PART = C_HALF // PARTS
 
 FLOPS = 2 * TOKENS * D * F * 2
 
@@ -87,14 +89,12 @@ def tile_dwamformer_pa_k_kernel(tc, x, w1_words, w1_scales, w2_words, w2_scales,
             return words
 
         def load_w2(piece):
-            first, first_half, end_half = piece
-            words = w2_pool.tile(
-                [P, W2_GROUPS, (end_half - first_half) * N_TILE], U32, name="w2_piece", align_bytes=64
-            )
+            first, count, first_half, end_half = piece
+            words = w2_pool.tile([P, count, (end_half - first_half) * N_TILE], U32, name="w2_piece", align_bytes=64)
             nc.sync.dma_start(
                 out=words[:].bitcast(I32),
                 in_=w2_rows[
-                    :, first : first + W2_GROUPS, first_half * N_TILE * PACK : end_half * N_TILE * PACK
+                    :, first : first + count, first_half * N_TILE * PACK : end_half * N_TILE * PACK
                 ].bitcast(I32),
             )
             return words
@@ -167,9 +167,14 @@ def tile_dwamformer_pa_k_kernel(tc, x, w1_words, w1_scales, w2_words, w2_scales,
                 in_=h_grouped[:].rearrange("p i w t -> p (i w t)"),
             )
 
-        pieces = [(first, 0, HALVES) for first in range(0, F_GROUPS - TAIL, W2_GROUPS)]
+        pieces = [(first, W2_GROUPS, 0, HALVES) for first in range(0, F_GROUPS - TAIL, W2_GROUPS)]
         for half in range(HALVES):
-            pieces.extend([(first, half, half + 1) for first in range(F_GROUPS - TAIL, F_GROUPS, W2_GROUPS)])
+            pieces.extend(
+                [(first, W2_GROUPS, half, half + 1) for first in range(F_GROUPS - TAIL, F_GROUPS, W2_GROUPS)]
+            )
+        first, count, first_half, end_half = pieces[-1]
+        pieces = pieces[:-1]
+        pieces.extend([(first + i, 1, first_half, end_half) for i in range(count)])
         w2_loaded = {}
         units_per_chunk = CHUNK // UNIT
         previous = None
@@ -191,32 +196,45 @@ def tile_dwamformer_pa_k_kernel(tc, x, w1_words, w1_scales, w2_words, w2_scales,
         transpose_and_quantise(UNITS - 1, previous)
 
         def pool_windows(half, a_bank):
-            chans = slice(half * C_HALF, (half + 1) * C_HALF)
-            gate = stage.tile([P, MS, C_HALF], F32, name="gate")
-            nc.scalar.activation(
-                out=gate[:], in_=a_bank[:].rearrange("p (c m) -> p m c", m=MS), func=ACT.Tanh, scale=0.5
-            )
-            expo = stage.tile([P, MS, C_HALF], F32, name="expo")
-            nc.scalar.activation(out=expo[:], in_=gate[:], func=ACT.Exp, scale=0.5)
-            weighted = stage.tile([P, MS, C_HALF], F32, name="weighted")
-            nc.vector.tensor_tensor(out=weighted[:], in0=expo[:], in1=x_tok[:, :, chans], op=ALU.mult)
-            top = stage.tile([P, C_HALF], F32, name="top")
-            nc.vector.tensor_reduce(
-                out=top[:], in_=weighted[:].rearrange("p m c -> p c m"), axis=mybir.AxisListType.X, op=ALU.add
-            )
-            bottom = stage.tile([P, C_HALF], F32, name="bottom")
-            nc.vector.tensor_reduce(
-                out=bottom[:], in_=expo[:].rearrange("p m c -> p c m"), axis=mybir.AxisListType.X, op=ALU.add
-            )
-            nc.vector.reciprocal(out=bottom[:], in_=bottom[:])
             result = stage.tile([P, C_HALF], F32, name="result")
-            nc.vector.tensor_tensor(out=result[:], in0=top[:], in1=bottom[:], op=ALU.mult)
-            nc.sync.dma_start(out=out_rows[:, chans], in_=result[:])
+            engines = (nc.gpsimd, nc.vector)
+            gates = []
+            for part in range(PARTS):
+                cols = slice(part * C_PART * MS, (part + 1) * C_PART * MS)
+                gate = stage.tile([P, MS, C_PART], F32, name="gate")
+                nc.scalar.activation(
+                    out=gate[:], in_=a_bank[:, cols].rearrange("p (c m) -> p m c", m=MS), func=ACT.Tanh, scale=0.5
+                )
+                gates.append(gate)
+            ready = []
+            for part, (gate, engine) in enumerate(zip(gates, engines)):
+                chans = slice(half * C_HALF + part * C_PART, half * C_HALF + (part + 1) * C_PART)
+                expo = stage.tile([P, MS, C_PART], F32, name="expo")
+                nc.scalar.activation(out=expo[:], in_=gate[:], func=ACT.Exp, scale=0.5)
+                weighted = stage.tile([P, MS, C_PART], F32, name="weighted")
+                engine.tensor_tensor(out=weighted[:], in0=expo[:], in1=x_tok[:, :, chans], op=ALU.mult)
+                bottom = stage.tile([P, C_PART], F32, name="bottom")
+                nc.vector.tensor_reduce(
+                    out=bottom[:], in_=expo[:].rearrange("p m c -> p c m"), axis=mybir.AxisListType.X, op=ALU.add
+                )
+                pairs = stage.tile([P, MS // 2, C_PART], F32, name="pairs")
+                engine.tensor_tensor(
+                    out=pairs[:], in0=weighted[:, 0 : MS // 2, :], in1=weighted[:, MS // 2 : MS, :], op=ALU.add
+                )
+                nc.vector.reciprocal(out=bottom[:], in_=bottom[:])
+                top = stage.tile([P, C_PART], F32, name="top")
+                engine.tensor_tensor(out=top[:], in0=pairs[:, 0, :], in1=pairs[:, 1, :], op=ALU.add)
+                ready.append((top, bottom))
+            for part, (top, bottom) in enumerate(ready):
+                nc.vector.tensor_tensor(
+                    out=result[:, part * C_PART : (part + 1) * C_PART], in0=top[:], in1=bottom[:], op=ALU.mult
+                )
+            nc.sync.dma_start(out=out_rows[:, half * C_HALF : (half + 1) * C_HALF], in_=result[:])
 
         a_banks = [psum_a.tile([P, N_TILE], F32, name="a_bank%d" % half) for half in range(HALVES)]
-        for index, (first, first_half, end_half) in enumerate(pieces):
+        for index, (first, count, first_half, end_half) in enumerate(pieces):
             words = w2_loaded[index]
-            for i in range(W2_GROUPS):
+            for i in range(count):
                 group = first + i
                 for half in range(first_half, end_half):
                     cols = slice((half - first_half) * N_TILE, (half - first_half + 1) * N_TILE)
@@ -233,6 +251,6 @@ def tile_dwamformer_pa_k_kernel(tc, x, w1_words, w1_scales, w2_words, w2_scales,
                     )
             if index + W2_BUFS < len(pieces):
                 w2_loaded[index + W2_BUFS] = load_w2(pieces[index + W2_BUFS])
-            if first + W2_GROUPS == F_GROUPS:
+            if first + count == F_GROUPS:
                 for half in range(first_half, end_half):
                     pool_windows(half, a_banks[half])

from contextlib import ExitStack

import concourse.mybir as mybir
from concourse.masks import make_identity

F32 = mybir.dt.float32
BF16 = mybir.dt.bfloat16
I32 = mybir.dt.int32
U32 = mybir.dt.uint32
U8 = mybir.dt.uint8
FP8X4 = mybir.dt.float8_e4m3fn_x4
ACT = mybir.ActivationFunctionType
ALU = mybir.AluOpType

P = 128
PACK = 4
K_PASS = P * PACK
N_TILE = 512

TOKENS = 128
MS = 4
C = 256
D = C * MS
F = D * 16
D_PASSES = D // K_PASS
F_GROUPS = F // K_PASS

QUADS = 4
PLANES = 4
ROWS = 4

UNIT = 2
UNITS = F_GROUPS // UNIT
CHUNK = 4
CHUNKS = F_GROUPS // CHUNK
W1_BUFS = 6
W2_GROUPS = 2
W2_BUFS = 8
TAIL = 8
HALVES = D // N_TILE
C_HALF = C // HALVES
PARTS = 2
C_PART = C_HALF // PARTS

FLOPS = 2 * TOKENS * D * F * 2


def tile_dwamformer_pa_k_kernel(tc, x, w1_words, w1_scales, w2_words, w2_scales, out):
    nc = tc.nc
    with ExitStack() as ctx:
        ctx.enter_context(tc.manual_schedule())
        keep = ctx.enter_context(tc.tile_pool(name="keep", bufs=1))
        w1_pool = ctx.enter_context(tc.tile_pool(name="w1_pool", bufs=W1_BUFS))
        w2_pool = ctx.enter_context(tc.tile_pool(name="w2_pool", bufs=W2_BUFS))
        stage = ctx.enter_context(tc.tile_pool(name="stage", bufs=2))
        psum_h = ctx.enter_context(tc.psum_pool(name="psum_h", bufs=2 * UNIT))
        psum_t = ctx.enter_context(tc.psum_pool(name="psum_t", bufs=2))
        psum_a = ctx.enter_context(tc.psum_pool(name="psum_a", bufs=1))

        x_rows = x.rearrange("b (w m) c -> (b w) m c", m=MS)
        w1_rows = w1_words.rearrange("g p n t -> p g (n t)")
        w2_rows = w2_words.rearrange("g p n t -> p g (n t)")
        out_rows = out.rearrange("b w c -> (b w) c")

        ident = keep.tile([P, P], BF16)
        x_tok = keep.tile([P, MS, C], BF16)
        flat_grouped = keep.tile([P, D_PASSES, TOKENS, PACK], BF16, align_bytes=64)
        flat_codes = keep.tile([P, D_PASSES, TOKENS], U32, align_bytes=64)
        flat_scales = keep.tile([P, D_PASSES, TOKENS], U8, align_bytes=64)
        h_codes = keep.tile([P, F_GROUPS, TOKENS], U32, align_bytes=64)
        h_scales = keep.tile([P, F_GROUPS, TOKENS], U8, align_bytes=64)
        w1_planes = keep.tile([P, D_PASSES, F // PLANES], U8, align_bytes=64)
        w2_planes = keep.tile([P, F_GROUPS // PLANES, D], U8, align_bytes=64)
        warm = keep.tile([P, 1], F32)

        nc.vector.memset(warm[:], 0.0)
        nc.vector.memset(w1_planes[:].bitcast(I32), 0)
        nc.vector.memset(w2_planes[:].bitcast(I32), 0)
        nc.scalar.activation(out=warm[:], in_=warm[:], func=ACT.Tanh)
        make_identity(nc, ident[:])

        def load_w1(chunk):
            words = w1_pool.tile([P, D_PASSES, CHUNK * N_TILE], U32, name="w1_chunk", align_bytes=64)
            first = chunk * CHUNK * N_TILE * PACK
            nc.sync.dma_start(
                out=words[:].bitcast(I32),
                in_=w1_rows[:, :, first : first + CHUNK * N_TILE * PACK].bitcast(I32),
            )
            return words

        def load_w2(piece):
            first, count, first_half, end_half = piece
            words = w2_pool.tile([P, count, (end_half - first_half) * N_TILE], U32, name="w2_piece", align_bytes=64)
            nc.sync.dma_start(
                out=words[:].bitcast(I32),
                in_=w2_rows[
                    :, first : first + count, first_half * N_TILE * PACK : end_half * N_TILE * PACK
                ].bitcast(I32),
            )
            return words

        def load_planes(planes, rows_of):
            for quad in range(QUADS):
                for r in range(ROWS):
                    first = 32 * quad + r
                    nc.sync.dma_start(
                        out=planes[first : first + PLANES * ROWS : ROWS, :, :].bitcast(I32),
                        in_=rows_of(ROWS * quad + r).bitcast(I32),
                    )

        nc.sync.dma_start(out=x_tok[:], in_=x_rows)
        w1_chunks = {}
        w1_chunks[0] = load_w1(0)
        load_planes(w1_planes, lambda q: w1_scales[:, q, :].rearrange("g (k n) -> k g n", k=PLANES))
        for chunk in range(1, W1_BUFS):
            w1_chunks[chunk] = load_w1(chunk)

        xt_bank = psum_t.tile([P, D_PASSES, MS, TOKENS], BF16, name="t_bank")
        for g in range(D_PASSES):
            for m in range(MS):
                nc.tensor.transpose(xt_bank[:, g, m, :], x_tok[:, m, g * P : (g + 1) * P], ident[:])
        nc.vector.tensor_copy(out=flat_grouped[:], in_=xt_bank[:].rearrange("p g m w -> p g w m"))
        nc.vector.quantize_mx(
            out=flat_codes[:].rearrange("p g w -> p (g w)").bitcast(FP8X4),
            scales=flat_scales[:].rearrange("p g w -> p (g w)"),
            in_=flat_grouped[:].rearrange("p g w m -> p (g w m)"),
        )

        def hidden(unit):
            h_sorted = stage.tile([P, UNIT, PACK, P], BF16, name="h_sorted")
            for i in range(UNIT):
                group = unit * UNIT + i
                words = w1_chunks[group // CHUNK]
                cols = slice((group % CHUNK) * N_TILE, (group % CHUNK + 1) * N_TILE)
                per_plane = F_GROUPS // PLANES
                plane = ROWS * (group // per_plane)
                plane_cols = slice((group % per_plane) * N_TILE, (group % per_plane + 1) * N_TILE)
                h_bank = psum_h.tile([P, N_TILE], F32, name="h_bank")
                for g in range(D_PASSES):
                    nc.tensor.matmul_mx(
                        out=h_bank[:],
                        lhsT=flat_codes[:, g, :].bitcast(FP8X4),
                        lhsT_scale=flat_scales[:, g, :],
                        rhs=words[:, g, cols].bitcast(FP8X4),
                        rhs_scale=w1_planes[plane:P, g, plane_cols],
                        start=(g == 0),
                        stop=(g == D_PASSES - 1),
                    )
                nc.scalar.activation(
                    out=h_sorted[:, i, :, :],
                    in_=h_bank[:].rearrange("p (q t) -> p t q", t=PACK),
                    func=ACT.Relu,
                )
            return h_sorted

        def transpose_and_quantise(unit, h_sorted):
            t_bank = psum_t.tile([P, UNIT, PACK, TOKENS], BF16, name="t_bank")
            for i in range(UNIT):
                for t in range(PACK):
                    nc.tensor.transpose(t_bank[:, i, t, :], h_sorted[:, i, t, :], ident[:])
            h_grouped = stage.tile([P, UNIT, TOKENS, PACK], BF16, name="h_grouped", align_bytes=64)
            nc.vector.tensor_copy(out=h_grouped[:], in_=t_bank[:].rearrange("p i t w -> p i w t"))
            groups = slice(unit * UNIT, (unit + 1) * UNIT)
            nc.vector.quantize_mx(
                out=h_codes[:, groups, :].rearrange("p i w -> p (i w)").bitcast(FP8X4),
                scales=h_scales[:, groups, :].rearrange("p i w -> p (i w)"),
                in_=h_grouped[:].rearrange("p i w t -> p (i w t)"),
            )

        pieces = [(first, W2_GROUPS, 0, HALVES) for first in range(0, F_GROUPS - TAIL, W2_GROUPS)]
        for half in range(HALVES):
            pieces.extend(
                [(first, W2_GROUPS, half, half + 1) for first in range(F_GROUPS - TAIL, F_GROUPS, W2_GROUPS)]
            )
        first, count, first_half, end_half = pieces[-1]
        pieces = pieces[:-1]
        pieces.extend([(first + i, 1, first_half, end_half) for i in range(count)])
        w2_loaded = {}
        units_per_chunk = CHUNK // UNIT
        previous = None
        for unit in range(UNITS):
            h_sorted = hidden(unit)
            if previous is not None:
                transpose_and_quantise(unit - 1, previous)
            previous = h_sorted
            if unit % units_per_chunk == units_per_chunk - 1:
                chunk = unit // units_per_chunk + W1_BUFS
                if chunk < CHUNKS:
                    w1_chunks[chunk] = load_w1(chunk)
                if chunk == CHUNKS - 1:
                    load_planes(
                        w2_planes, lambda q: w2_scales[:, q, :].rearrange("(a k) n -> k a n", k=PLANES)
                    )
                    for index in range(W2_BUFS):
                        w2_loaded[index] = load_w2(pieces[index])
        transpose_and_quantise(UNITS - 1, previous)

        def pool_windows(half, a_bank):
            result = stage.tile([P, C_HALF], F32, name="result")
            engines = (nc.gpsimd, nc.vector)
            gates = []
            for part in range(PARTS):
                cols = slice(part * C_PART * MS, (part + 1) * C_PART * MS)
                gate = stage.tile([P, MS, C_PART], F32, name="gate")
                nc.scalar.activation(
                    out=gate[:], in_=a_bank[:, cols].rearrange("p (c m) -> p m c", m=MS), func=ACT.Tanh, scale=0.5
                )
                gates.append(gate)
            ready = []
            for part, (gate, engine) in enumerate(zip(gates, engines)):
                chans = slice(half * C_HALF + part * C_PART, half * C_HALF + (part + 1) * C_PART)
                expo = stage.tile([P, MS, C_PART], F32, name="expo")
                nc.scalar.activation(out=expo[:], in_=gate[:], func=ACT.Exp, scale=0.5)
                weighted = stage.tile([P, MS, C_PART], F32, name="weighted")
                engine.tensor_tensor(out=weighted[:], in0=expo[:], in1=x_tok[:, :, chans], op=ALU.mult)
                bottom = stage.tile([P, C_PART], F32, name="bottom")
                nc.vector.tensor_reduce(
                    out=bottom[:], in_=expo[:].rearrange("p m c -> p c m"), axis=mybir.AxisListType.X, op=ALU.add
                )
                pairs = stage.tile([P, MS // 2, C_PART], F32, name="pairs")
                engine.tensor_tensor(
                    out=pairs[:], in0=weighted[:, 0 : MS // 2, :], in1=weighted[:, MS // 2 : MS, :], op=ALU.add
                )
                nc.vector.reciprocal(out=bottom[:], in_=bottom[:])
                top = stage.tile([P, C_PART], F32, name="top")
                engine.tensor_tensor(out=top[:], in0=pairs[:, 0, :], in1=pairs[:, 1, :], op=ALU.add)
                ready.append((top, bottom))
            for part, (top, bottom) in enumerate(ready):
                nc.vector.tensor_tensor(
                    out=result[:, part * C_PART : (part + 1) * C_PART], in0=top[:], in1=bottom[:], op=ALU.mult
                )
            nc.sync.dma_start(out=out_rows[:, half * C_HALF : (half + 1) * C_HALF], in_=result[:])

        a_banks = [psum_a.tile([P, N_TILE], F32, name="a_bank%d" % half) for half in range(HALVES)]
        for index, (first, count, first_half, end_half) in enumerate(pieces):
            words = w2_loaded[index]
            for i in range(count):
                group = first + i
                for half in range(first_half, end_half):
                    cols = slice((half - first_half) * N_TILE, (half - first_half + 1) * N_TILE)
                    nc.tensor.matmul_mx(
                        out=a_banks[half][:],
                        lhsT=h_codes[:, group, :].bitcast(FP8X4),
                        lhsT_scale=h_scales[:, group, :],
                        rhs=words[:, i, cols].bitcast(FP8X4),
                        rhs_scale=w2_planes[
                            ROWS * (group % PLANES) : P, group // PLANES, half * N_TILE : (half + 1) * N_TILE
                        ],
                        start=(group == 0),
                        stop=(group == F_GROUPS - 1),
                    )
            if index + W2_BUFS < len(pieces):
                w2_loaded[index + W2_BUFS] = load_w2(pieces[index + W2_BUFS])
            if first + count == F_GROUPS:
                for half in range(first_half, end_half):
                    pool_windows(half, a_banks[half])
